import numpy as np
import ml_dtypes


def mxq(x, axis, fmt="e4m3"):
    dtype, down = {"e4m3": (ml_dtypes.float8_e4m3fn, 7), "e5m2": (ml_dtypes.float8_e5m2, 14)}[fmt]
    v = np.moveaxis(np.asarray(x, np.float32).astype(ml_dtypes.bfloat16).astype(np.float64), axis, -1)
    blocks = v.reshape(v.shape[:-1] + (-1, 32))
    amax = np.abs(blocks).max(-1, keepdims=True)
    byte = np.maximum(np.where(amax > 0, np.frexp(amax)[1] - 1 + 127, 0) - down, 1)
    scale = np.exp2(byte - 127.0)
    codes = (blocks / scale).astype(np.float32).astype(dtype).astype(np.float64)
    return np.moveaxis((codes * scale).reshape(v.shape), -1, axis)


WIDE = False


def mx_kscale(k):
    if not WIDE:
        return np.ones(k)
    levels = np.array([10, -10, 5, -5, 0])
    a = np.random.permutation(np.resize(levels, k // 512 * 4)).reshape(k // 512, 4)
    idx = np.arange(k)
    return np.exp2(a[idx // 512, idx % 128 // 32])


BF16 = ml_dtypes.bfloat16


def bf(x):
    return np.asarray(x, np.float32).astype(BF16)


def f64(x):
    return np.asarray(x).astype(np.float64)


B, PED, NED, CED = 6144, 320, 128, 512
Q = PED // 4
FEAT = 2 * PED + 3 * NED


def leaky(v):
    return np.where(v >= 0.0, v, 0.01 * v)


def point_enc(xy, wsx, bsx, wcx, bcx, wsy, bsy, wcy, bcy):
    x = xy[:, 0:1]
    y = xy[:, 1:2]
    return np.concatenate([np.sin(x * wsx + bsx), np.cos(x * wcx + bcx), np.sin(y * wsy + bsy), np.cos(y * wcy + bcy)], axis=-1)


def num_enc(t, w, b):
    return leaky(t[:, None] * w + b)


def setup_inputs():
    s = np.array(mx_kscale(FEAT), dtype=np.float64)
    s[:2 * PED] = 1.0
    t = mx_kscale(CED)
    d = {'src_xy': bf(np.random.standard_normal((B, 2))), 'dst_xy': bf(np.random.standard_normal((B, 2))),
         'time_s': bf(np.random.uniform(size=B)), 'wait_src': bf(np.random.uniform(size=B)), 'wait_dst': bf(np.random.uniform(size=B))}
    for pfx in ('src', 'dst'):
        for part in ('wsx', 'bsx', 'wcx', 'bcx', 'wsy', 'bsy', 'wcy', 'bcy'):
            d[pfx + '_' + part] = bf(np.random.standard_normal(Q) * (1.0 if part[0] == 'w' else 0.1))
    for i, pfx in enumerate(('t', 'ws', 'wd')):
        sn = s[2 * PED + i * NED:2 * PED + (i + 1) * NED]
        d[pfx + '_w'] = bf(np.random.standard_normal(NED) * sn)
        d[pfx + '_b'] = bf(np.random.standard_normal(NED) * 0.1 * sn)
    d['W1'] = bf(np.random.standard_normal((FEAT, CED)) * 1.5 / np.sqrt(FEAT) / s[:, None] * t[None, :])
    d['b1'] = bf(np.random.standard_normal(CED) * 0.1 * t)
    d['W2'] = bf(np.random.standard_normal((CED, CED)) * 1.5 / np.sqrt(CED) / t[:, None])
    d['b2'] = bf(np.random.standard_normal(CED) * 0.1)
    return d


def reference(src_xy, dst_xy, time_s, wait_src, wait_dst,
              src_wsx, src_bsx, src_wcx, src_bcx, src_wsy, src_bsy, src_wcy, src_bcy,
              dst_wsx, dst_bsx, dst_wcx, dst_bcx, dst_wsy, dst_bsy, dst_wcy, dst_bcy,
              t_w, t_b, ws_w, ws_b, wd_w, wd_b,
              W1, b1, W2, b2):
    feats = np.concatenate([
        point_enc(f64(src_xy), f64(src_wsx), f64(src_bsx), f64(src_wcx), f64(src_bcx),
                        f64(src_wsy), f64(src_bsy), f64(src_wcy), f64(src_bcy)),
        point_enc(f64(dst_xy), f64(dst_wsx), f64(dst_bsx), f64(dst_wcx), f64(dst_bcx),
                        f64(dst_wsy), f64(dst_bsy), f64(dst_wcy), f64(dst_bcy)),
        num_enc(f64(time_s), f64(t_w), f64(t_b)),
        num_enc(f64(wait_src), f64(ws_w), f64(ws_b)),
        num_enc(f64(wait_dst), f64(wd_w), f64(wd_b)),
    ], axis=-1)
    h = leaky((mxq(feats, 1, 'e4m3') @ mxq(f64(W1), 0, 'e4m3')) + f64(b1))
    return leaky((mxq(h, 1, 'e4m3') @ mxq(f64(W2), 0, 'e4m3')) + f64(b2))

@@ -1,0 +1,199 @@
+import math
+from contextlib import ExitStack
+
+import concourse.mybir as mybir
+from concourse.masks import make_identity
+
+FLOPS = 2 * 6144 * (1024 * 512 + 512 * 512)
+
+F32 = mybir.dt.float32
+BF16 = mybir.dt.bfloat16
+I32 = mybir.dt.int32
+U32 = mybir.dt.uint32
+U8 = mybir.dt.uint8
+FP8X4 = mybir.dt.float8_e4m3fn_x4
+ALU = mybir.AluOpType
+ACT = mybir.ActivationFunctionType
+
+P = 128
+B = 6144
+F = 1024
+NT = 512
+H = 512
+TWO_PI = 2.0 * math.pi
+
+REGROUP_A_ON_SCALAR = True
+NUM_AFFINE_ON_SCALAR = True
+
+
+def tile_claimencoder_t_kernel(
+    tc, src_xy, dst_xy, time_s, wait_src, wait_dst,
+    src_wsx, src_bsx, src_wcx, src_bcx, src_wsy, src_bsy, src_wcy, src_bcy,
+    dst_wsx, dst_bsx, dst_wcx, dst_bcx, dst_wsy, dst_bsy, dst_wcy, dst_bcy,
+    t_w, t_b, ws_w, ws_b, wd_w, wd_b, W1, b1, W2, b2, out,
+):
+    nc = tc.nc
+    with ExitStack() as ctx:
+        const = ctx.enter_context(tc.tile_pool(name="const", bufs=1))
+        ps1 = ctx.enter_context(tc.psum_pool(name="ps1", bufs=4))
+        ps2 = ctx.enter_context(tc.psum_pool(name="ps2", bufs=4))
+
+        wsin = const.tile([P, 5], BF16)
+        bsin = const.tile([P, 5], BF16)
+        w_vecs = (src_wsx, src_wcx, src_wsy, src_wcy, dst_wsx, dst_wcx, dst_wsy, dst_wcy)
+        b_vecs = (src_bsx, src_bcx, src_bsy, src_bcy, dst_bsx, dst_bcx, dst_bsy, dst_bcy)
+        for g in range(8):
+            nc.sync.dma_start(out=wsin[16 * g:16 * g + 16, :], in_=w_vecs[g].rearrange("(r s) -> r s", s=5))
+            nc.scalar.dma_start(out=bsin[16 * g:16 * g + 16, :], in_=b_vecs[g].rearrange("(r s) -> r s", s=5))
+
+        ident = const.tile([P, P], BF16)
+        make_identity(nc, ident[:])
+        rows = const.tile([P, P], BF16)
+        nc.vector.memset(rows[:], 0.0)
+        nc.vector.memset(rows[32:33, :].rearrange("o (g h r) -> o g h r", h=2, r=16)[:, :, 1, :], 1.0)
+        for i, v in enumerate((t_w, ws_w, wd_w, t_b, ws_b, wd_b)):
+            nc.gpsimd.dma_start(out=rows[i:i + 1, :], in_=v.rearrange("(o n) -> o n", o=1))
+        nc.gpsimd.dma_start(out=rows[6:10, :], in_=b1.rearrange("(t p) -> t p", p=P))
+        b2bc = const.tile([P, H], BF16)
+        nc.gpsimd.dma_start(out=b2bc[:], in_=b2.partition_broadcast(P))
+
+        cols_ps = ps2.tile([P, P], BF16, tag="l2")
+        nc.tensor.transpose(cols_ps[:], rows[:], ident[:])
+        prm = const.tile([P, 40], F32)
+        nc.vector.tensor_copy(out=prm[:, 0:33], in_=cols_ps[:, 0:33])
+
+        wt = const.tile([P, 5], F32)
+        nc.vector.tensor_scalar(out=wt[:], in0=wsin[:], scalar1=1.0 / TWO_PI, scalar2=None, op0=ALU.mult)
+        quarter = const.tile([P, 1], F32)
+        nc.vector.tensor_scalar(out=quarter[:], in0=prm[:, 32:33], scalar1=0.25, scalar2=None, op0=ALU.mult)
+        halfpi = const.tile([P, 1], F32)
+        nc.vector.tensor_scalar(out=halfpi[:], in0=prm[:, 32:33], scalar1=0.5 * math.pi, scalar2=None, op0=ALU.mult)
+        bt = const.tile([P, 5], F32)
+        nc.vector.tensor_scalar(out=bt[:], in0=bsin[:], scalar1=1.0 / TWO_PI, scalar2=quarter[:, 0:1], op0=ALU.mult, op1=ALU.add)
+        beta = const.tile([P, 5], F32)
+        nc.vector.tensor_scalar(out=beta[:], in0=bsin[:], scalar1=halfpi[:, 0:1], scalar2=None, op0=ALU.add)
+
+        w1c = const.tile([P, 3, H], U32, align_bytes=64)
+        w1s = const.tile([P, 3, H], U8, align_bytes=64)
+        w2c = const.tile([P, H], U32, align_bytes=64)
+        w2s = const.tile([P, H], U8, align_bytes=64)
+        with tc.tile_pool(name="stage", bufs=1) as stage:
+            w1sin = stage.tile([P, 5, H], BF16)
+            nc.sync.dma_start(out=w1sin[:], in_=W1[0:640, :].rearrange("(p s) n -> p s n", s=5))
+            w1num = stage.tile([P, 3, H], BF16)
+            nc.sync.dma_start(out=w1num[:], in_=W1[640:1024, :].rearrange("(i p) n -> p i n", p=P))
+            w2raw = stage.tile([P, 4, H], BF16)
+            nc.sync.dma_start(out=w2raw[:], in_=W2.rearrange("(t p) n -> p t n", p=P))
+            gwa = stage.tile([P, H, 4], BF16, align_bytes=64)
+            gwb = stage.tile([P, H, 4], BF16, align_bytes=64)
+            gwc = stage.tile([P, H, 4], BF16, align_bytes=64)
+            gw2 = stage.tile([P, H, 4], BF16, align_bytes=64)
+            nc.vector.memset(gwb[:], 0.0)
+            nc.vector.memset(gwc[:], 0.0)
+            nc.scalar.copy(out=gwa[:], in_=w1sin[:, 0:4, :].rearrange("p t n -> p n t"))
+            nc.scalar.copy(out=gwb[:, :, 0], in_=w1sin[:, 4, :])
+            nc.scalar.copy(out=gwc[:, :, 0:3], in_=w1num[:].rearrange("p i n -> p n i"))
+            nc.scalar.copy(out=gw2[:], in_=w2raw[:].rearrange("p t n -> p n t"))
+            for q, gw in enumerate((gwa, gwb, gwc)):
+                nc.vector.quantize_mx(out=w1c[:, q, :].bitcast(FP8X4), scales=w1s[:, q, :],
+                                      in_=gw[:].rearrange("p n t -> p (n t)"))
+            nc.vector.quantize_mx(out=w2c[:].bitcast(FP8X4), scales=w2s[:],
+                                  in_=gw2[:].rearrange("p n t -> p (n t)"))
+
+        outp = ctx.enter_context(tc.tile_pool(name="outp", bufs=3))
+        hid = ctx.enter_context(tc.tile_pool(name="hid", bufs=2))
+        inp = ctx.enter_context(tc.tile_pool(name="inp", bufs=2))
+        work = ctx.enter_context(tc.tile_pool(name="work", bufs=2))
+        codes = ctx.enter_context(tc.tile_pool(name="codes", bufs=2))
+
+        g_b = []
+        g_c = []
+        for k in range(1):
+            gb = const.tile([P, F, 4], BF16, name="gb%d" % k, align_bytes=64)
+            nc.vector.memset(gb[:], 0.0)
+            g_b.append(gb)
+            gc = const.tile([P, F, 4], BF16, name="gc%d" % k, align_bytes=64)
+            nc.vector.memset(gc[:], 0.0)
+            g_c.append(gc)
+
+        src_flat = src_xy.rearrange("b c -> (b c)")
+        dst_flat = dst_xy.rearrange("b c -> (b c)")
+
+        for c in range(B // F):
+            xy = inp.tile([P, 2 * F], BF16, tag="xy")
+            for q, (flat, off) in enumerate(((src_flat, 0), (src_flat, 1), (dst_flat, 0), (dst_flat, 1))):
+                n_el = 2 * F - off
+                lo = 2 * F * c + off
+                nc.sync.dma_start(out=xy[32 * q:32 * q + 32, 0:n_el], in_=flat[lo:lo + n_el].partition_broadcast(32))
+            tin = inp.tile([P, 3, F], BF16, tag="tin")
+            for i, v in enumerate((time_s, wait_src, wait_dst)):
+                nc.sync.dma_start(out=tin[:, i, :], in_=v[F * c:F * c + F].partition_broadcast(P))
+            xv = xy[:].rearrange("p (b c) -> p b c", c=2)[:, :, 0]
+
+            planes = work.tile([P, 4, F], BF16, tag="planes")
+            gb = g_b[0]
+            gc = g_c[0]
+            for s in range(5):
+                n_t = work.tile([P, F], I32, tag="n")
+                nc.vector.tensor_scalar(out=n_t[:], in0=xv, scalar1=wt[:, s:s + 1], scalar2=bt[:, s:s + 1],
+                                        op0=ALU.mult, op1=ALU.add)
+                f_t = work.tile([P, F], F32, tag="f", bufs=3)
+                nc.vector.scalar_tensor_tensor(out=f_t[:], in0=xv, scalar=wt[:, s:s + 1], in1=n_t[:],
+                                               op0=ALU.mult, op1=ALU.subtract)
+                dst = planes[:, s, :] if s < 4 else gb[:, :, 0]
+                nc.scalar.activation(out=dst, in_=f_t[:], func=ACT.Sin, bias=beta[:, s:s + 1], scale=TWO_PI)
+            ga = work.tile([P, F, 4], BF16, tag="ga", align_bytes=64)
+            if REGROUP_A_ON_SCALAR:
+                nc.scalar.copy(out=ga[:], in_=planes[:].rearrange("p t b -> p b t"))
+            else:
+                nc.vector.tensor_copy(out=ga[:], in_=planes[:].rearrange("p t b -> p b t"))
+
+            a_t = work.tile([P, 3, F], F32, tag="a")
+            for i in range(3):
+                if NUM_AFFINE_ON_SCALAR:
+                    nc.scalar.activation(out=a_t[:, i, :], in_=tin[:, i, :], func=ACT.Identity,
+                                         bias=prm[:, 3 + i:4 + i], scale=prm[:, i:i + 1])
+                else:
+                    nc.vector.tensor_scalar(out=a_t[:, i, :], in0=tin[:, i, :], scalar1=prm[:, i:i + 1],
+                                            scalar2=prm[:, 3 + i:4 + i], op0=ALU.mult, op1=ALU.add)
+            a_v = a_t[:].rearrange("p i b -> p b i")
+            nc.vector.scalar_tensor_tensor(out=gc[:, :, 0:3], in0=a_v, scalar=0.01, in1=a_v,
+                                           op0=ALU.mult, op1=ALU.max)
+
+            fcs = []
+            fss = []
+            for q, g in enumerate((ga, gb, gc)):
+                fc = codes.tile([P, F], U32, name="fc%d" % q, align_bytes=64)
+                fs = codes.tile([P, F], U8, name="fs%d" % q, align_bytes=64)
+                nc.vector.quantize_mx(out=fc[:].bitcast(FP8X4), scales=fs[:], in_=g[:].rearrange("p b t -> p (b t)"))
+                fcs.append(fc)
+                fss.append(fs)
+
+            for half in range(F // NT):
+                j = c * (F // NT) + half
+                cs = slice(NT * half, NT * half + NT)
+                apl = hid.tile([P, 4, NT], F32, tag="apl")
+                for t in range(4):
+                    acc = ps1.tile([P, NT], F32, tag="l1")
+                    ms = slice(P * t, P * t + P)
+                    for q in range(3):
+                        nc.tensor.matmul_mx(out=acc[:], lhsT=w1c[:, q, ms].bitcast(FP8X4), lhsT_scale=w1s[:, q, ms],
+                                            rhs=fcs[q][:, cs].bitcast(FP8X4), rhs_scale=fss[q][:, cs],
+                                            start=(q == 0), stop=(q == 2))
+                    nc.scalar.activation(out=apl[:, t, :], in_=acc[:], func=ACT.Identity,
+                                         bias=prm[:, 6 + t:7 + t], scale=1.0)
+                hg = hid.tile([P, NT, 4], BF16, tag="hg", align_bytes=64)
+                apv = apl[:].rearrange("p t b -> p b t")
+                nc.vector.scalar_tensor_tensor(out=hg[:], in0=apv, scalar=0.01, in1=apv, op0=ALU.mult, op1=ALU.max)
+                hc = hid.tile([P, NT], U32, tag="hc", align_bytes=64)
+                hs = hid.tile([P, NT], U8, tag="hs", align_bytes=64)
+                nc.vector.quantize_mx(out=hc[:].bitcast(FP8X4), scales=hs[:], in_=hg[:].rearrange("p b t -> p (b t)"))
+                o1 = outp.tile([P, 4, H], F32, tag="o1")
+                for i in range(4):
+                    acc2 = ps2.tile([P, H], F32, tag="l2")
+                    ms = slice(P * i, P * i + P)
+                    nc.tensor.matmul_mx(out=acc2[:], lhsT=hc[:, ms].bitcast(FP8X4), lhsT_scale=hs[:, ms],
+                                        rhs=w2c[:].bitcast(FP8X4), rhs_scale=w2s[:], start=True, stop=True)
+                    nc.vector.tensor_tensor(out=o1[:, i, :], in0=acc2[:], in1=b2bc[:], op=ALU.add)
+                nc.vector.scalar_tensor_tensor(out=o1[:], in0=o1[:], scalar=0.01, in1=o1[:], op0=ALU.mult, op1=ALU.max)
+                nc.sync.dma_start(out=out[NT * j:NT * j + NT, :].rearrange("(i p) n -> p i n", p=P), in_=o1[:])

@@ -20,10 +20,8 @@ B = 6144
 F = 1024
 NT = 512
 H = 512
+NCH = B // F
 TWO_PI = 2.0 * math.pi
-
-REGROUP_A_ON_SCALAR = True
-NUM_AFFINE_ON_SCALAR = True
 
 
 def tile_claimencoder_t_kernel(
@@ -34,9 +32,44 @@ def tile_claimencoder_t_kernel(
 ):
     nc = tc.nc
     with ExitStack() as ctx:
+        ctx.enter_context(tc.manual_schedule())
         const = ctx.enter_context(tc.tile_pool(name="const", bufs=1))
         ps1 = ctx.enter_context(tc.psum_pool(name="ps1", bufs=4))
         ps2 = ctx.enter_context(tc.psum_pool(name="ps2", bufs=4))
+        stage = ctx.enter_context(tc.tile_pool(name="stage", bufs=1))
+        outp = ctx.enter_context(tc.tile_pool(name="outp", bufs=3))
+        hid = ctx.enter_context(tc.tile_pool(name="hid", bufs=2))
+        inp = ctx.enter_context(tc.tile_pool(name="inp", bufs=2))
+        work = ctx.enter_context(tc.tile_pool(name="work", bufs=2))
+        codes = ctx.enter_context(tc.tile_pool(name="codes", bufs=2))
+
+        src_flat = src_xy.rearrange("b c -> (b c)")
+        dst_flat = dst_xy.rearrange("b c -> (b c)")
+        xy_t = {}
+        tin_t = {}
+
+        def load_xy(c):
+            xy = inp.tile([P, 2 * F], BF16, tag="xy", name="xy")
+            for q, (flat, off) in enumerate(((src_flat, 0), (src_flat, 1), (dst_flat, 0), (dst_flat, 1))):
+                n_el = 2 * F - off
+                lo = 2 * F * c + off
+                nc.sync.dma_start(out=xy[32 * q:32 * q + 32, 0:n_el], in_=flat[lo:lo + n_el].partition_broadcast(32))
+            xy_t[c] = xy
+
+        def load_tin(c):
+            tin = inp.tile([P, 3, F], BF16, tag="tin", name="tin")
+            for i, v in enumerate((time_s, wait_src, wait_dst)):
+                nc.sync.dma_start(out=tin[:, i, :], in_=v[F * c:F * c + F].partition_broadcast(P))
+            tin_t[c] = tin
+
+        ident = const.tile([P, P], BF16)
+        make_identity(nc, ident[:])
+        w1sin = stage.tile([P, 5, H], BF16)
+        nc.gpsimd.dma_start(out=w1sin[:], in_=W1[0:640, :].rearrange("(p s) n -> p s n", s=5))
+        w1num = stage.tile([P, 3, H], BF16)
+        nc.gpsimd.dma_start(out=w1num[:], in_=W1[640:1024, :].rearrange("(i p) n -> p i n", p=P))
+        w2raw = stage.tile([P, 4, H], BF16)
+        nc.gpsimd.dma_start(out=w2raw[:], in_=W2.rearrange("(t p) n -> p t n", p=P))
 
         wsin = const.tile([P, 5], BF16)
         bsin = const.tile([P, 5], BF16)
@@ -45,29 +78,42 @@ def tile_claimencoder_t_kernel(
         for g in range(8):
             nc.sync.dma_start(out=wsin[16 * g:16 * g + 16, :], in_=w_vecs[g].rearrange("(r s) -> r s", s=5))
             nc.scalar.dma_start(out=bsin[16 * g:16 * g + 16, :], in_=b_vecs[g].rearrange("(r s) -> r s", s=5))
+        load_xy(0)
 
-        ident = const.tile([P, P], BF16)
-        make_identity(nc, ident[:])
+        mark = const.tile([P, P], BF16)
+        nc.vector.memset(mark[:], 0.0)
+        nc.vector.memset(mark[0:1, :].rearrange("o (g h r) -> o g h r", h=2, r=16)[:, :, 1, :], 1.0)
         rows = const.tile([P, P], BF16)
         nc.vector.memset(rows[:], 0.0)
-        nc.vector.memset(rows[32:33, :].rearrange("o (g h r) -> o g h r", h=2, r=16)[:, :, 1, :], 1.0)
         for i, v in enumerate((t_w, ws_w, wd_w, t_b, ws_b, wd_b)):
-            nc.gpsimd.dma_start(out=rows[i:i + 1, :], in_=v.rearrange("(o n) -> o n", o=1))
-        nc.gpsimd.dma_start(out=rows[6:10, :], in_=b1.rearrange("(t p) -> t p", p=P))
+            nc.scalar.dma_start(out=rows[i:i + 1, :], in_=v.rearrange("(o n) -> o n", o=1))
+        nc.scalar.dma_start(out=rows[6:10, :], in_=b1.rearrange("(t p) -> t p", p=P))
+        load_tin(0)
         b2bc = const.tile([P, H], BF16)
-        nc.gpsimd.dma_start(out=b2bc[:], in_=b2.partition_broadcast(P))
+        nc.sync.dma_start(out=b2bc[:], in_=b2.partition_broadcast(P))
 
-        cols_ps = ps2.tile([P, P], BF16, tag="l2")
-        nc.tensor.transpose(cols_ps[:], rows[:], ident[:])
-        prm = const.tile([P, 40], F32)
-        nc.vector.tensor_copy(out=prm[:, 0:33], in_=cols_ps[:, 0:33])
+        mark_ps = ps2.tile([P, P], BF16, tag="l2")
+        nc.tensor.transpose(mark_ps[:], mark[:], ident[:])
+        is_cos = const.tile([P, 1], F32)
+        nc.vector.tensor_copy(out=is_cos[:], in_=mark_ps[:, 0:1])
+        quarter = const.tile([P, 1], F32)
+        nc.vector.tensor_scalar(out=quarter[:], in0=is_cos[:], scalar1=0.25, scalar2=None, op0=ALU.mult)
+        halfpi = const.tile([P, 1], F32)
+        nc.vector.tensor_scalar(out=halfpi[:], in0=is_cos[:], scalar1=0.5 * math.pi, scalar2=None, op0=ALU.mult)
+
+        gb = const.tile([P, F, 4], BF16, align_bytes=64)
+        nc.vector.memset(gb[:], 0.0)
+        gc = const.tile([P, F, 4], BF16, align_bytes=64)
+        nc.vector.memset(gc[:], 0.0)
+        gwa = stage.tile([P, H, 4], BF16, align_bytes=64)
+        gwb = stage.tile([P, H, 4], BF16, align_bytes=64)
+        gwc = stage.tile([P, H, 4], BF16, align_bytes=64)
+        gw2 = stage.tile([P, H, 4], BF16, align_bytes=64)
+        nc.vector.memset(gwb[:], 0.0)
+        nc.vector.memset(gwc[:], 0.0)
 
         wt = const.tile([P, 5], F32)
         nc.vector.tensor_scalar(out=wt[:], in0=wsin[:], scalar1=1.0 / TWO_PI, scalar2=None, op0=ALU.mult)
-        quarter = const.tile([P, 1], F32)
-        nc.vector.tensor_scalar(out=quarter[:], in0=prm[:, 32:33], scalar1=0.25, scalar2=None, op0=ALU.mult)
-        halfpi = const.tile([P, 1], F32)
-        nc.vector.tensor_scalar(out=halfpi[:], in0=prm[:, 32:33], scalar1=0.5 * math.pi, scalar2=None, op0=ALU.mult)
         bt = const.tile([P, 5], F32)
         nc.vector.tensor_scalar(out=bt[:], in0=bsin[:], scalar1=1.0 / TWO_PI, scalar2=quarter[:, 0:1], op0=ALU.mult, op1=ALU.add)
         beta = const.tile([P, 5], F32)
@@ -77,123 +123,221 @@ def tile_claimencoder_t_kernel(
         w1s = const.tile([P, 3, H], U8, align_bytes=64)
         w2c = const.tile([P, H], U32, align_bytes=64)
         w2s = const.tile([P, H], U8, align_bytes=64)
-        with tc.tile_pool(name="stage", bufs=1) as stage:
-            w1sin = stage.tile([P, 5, H], BF16)
-            nc.sync.dma_start(out=w1sin[:], in_=W1[0:640, :].rearrange("(p s) n -> p s n", s=5))
-            w1num = stage.tile([P, 3, H], BF16)
-            nc.sync.dma_start(out=w1num[:], in_=W1[640:1024, :].rearrange("(i p) n -> p i n", p=P))
-            w2raw = stage.tile([P, 4, H], BF16)
-            nc.sync.dma_start(out=w2raw[:], in_=W2.rearrange("(t p) n -> p t n", p=P))
-            gwa = stage.tile([P, H, 4], BF16, align_bytes=64)
-            gwb = stage.tile([P, H, 4], BF16, align_bytes=64)
-            gwc = stage.tile([P, H, 4], BF16, align_bytes=64)
-            gw2 = stage.tile([P, H, 4], BF16, align_bytes=64)
-            nc.vector.memset(gwb[:], 0.0)
-            nc.vector.memset(gwc[:], 0.0)
-            nc.scalar.copy(out=gwa[:], in_=w1sin[:, 0:4, :].rearrange("p t n -> p n t"))
-            nc.scalar.copy(out=gwb[:, :, 0], in_=w1sin[:, 4, :])
-            nc.scalar.copy(out=gwc[:, :, 0:3], in_=w1num[:].rearrange("p i n -> p n i"))
-            nc.scalar.copy(out=gw2[:], in_=w2raw[:].rearrange("p t n -> p n t"))
-            for q, gw in enumerate((gwa, gwb, gwc)):
-                nc.vector.quantize_mx(out=w1c[:, q, :].bitcast(FP8X4), scales=w1s[:, q, :],
-                                      in_=gw[:].rearrange("p n t -> p (n t)"))
-            nc.vector.quantize_mx(out=w2c[:].bitcast(FP8X4), scales=w2s[:],
-                                  in_=gw2[:].rearrange("p n t -> p (n t)"))
+        prm = const.tile([P, 16], F32)
 
-        outp = ctx.enter_context(tc.tile_pool(name="outp", bufs=3))
-        hid = ctx.enter_context(tc.tile_pool(name="hid", bufs=2))
-        inp = ctx.enter_context(tc.tile_pool(name="inp", bufs=2))
-        work = ctx.enter_context(tc.tile_pool(name="work", bufs=2))
-        codes = ctx.enter_context(tc.tile_pool(name="codes", bufs=2))
-
-        g_b = []
-        g_c = []
-        for k in range(1):
-            gb = const.tile([P, F, 4], BF16, name="gb%d" % k, align_bytes=64)
-            nc.vector.memset(gb[:], 0.0)
-            g_b.append(gb)
-            gc = const.tile([P, F, 4], BF16, name="gc%d" % k, align_bytes=64)
-            nc.vector.memset(gc[:], 0.0)
-            g_c.append(gc)
-
-        src_flat = src_xy.rearrange("b c -> (b c)")
-        dst_flat = dst_xy.rearrange("b c -> (b c)")
-
-        for c in range(B // F):
-            xy = inp.tile([P, 2 * F], BF16, tag="xy")
-            for q, (flat, off) in enumerate(((src_flat, 0), (src_flat, 1), (dst_flat, 0), (dst_flat, 1))):
-                n_el = 2 * F - off
-                lo = 2 * F * c + off
-                nc.sync.dma_start(out=xy[32 * q:32 * q + 32, 0:n_el], in_=flat[lo:lo + n_el].partition_broadcast(32))
-            tin = inp.tile([P, 3, F], BF16, tag="tin")
-            for i, v in enumerate((time_s, wait_src, wait_dst)):
-                nc.sync.dma_start(out=tin[:, i, :], in_=v[F * c:F * c + F].partition_broadcast(P))
-            xv = xy[:].rearrange("p (b c) -> p b c", c=2)[:, :, 0]
-
-            planes = work.tile([P, 4, F], BF16, tag="planes")
-            gb = g_b[0]
-            gc = g_c[0]
-            for s in range(5):
-                n_t = work.tile([P, F], I32, tag="n")
-                nc.vector.tensor_scalar(out=n_t[:], in0=xv, scalar1=wt[:, s:s + 1], scalar2=bt[:, s:s + 1],
-                                        op0=ALU.mult, op1=ALU.add)
-                f_t = work.tile([P, F], F32, tag="f", bufs=3)
-                nc.vector.scalar_tensor_tensor(out=f_t[:], in0=xv, scalar=wt[:, s:s + 1], in1=n_t[:],
-                                               op0=ALU.mult, op1=ALU.subtract)
-                dst = planes[:, s, :] if s < 4 else gb[:, :, 0]
-                nc.scalar.activation(out=dst, in_=f_t[:], func=ACT.Sin, bias=beta[:, s:s + 1], scale=TWO_PI)
-            ga = work.tile([P, F, 4], BF16, tag="ga", align_bytes=64)
-            if REGROUP_A_ON_SCALAR:
-                nc.scalar.copy(out=ga[:], in_=planes[:].rearrange("p t b -> p b t"))
+        def weight_regroup(k):
+            if k == 0:
+                nc.scalar.copy(out=gwa[:], in_=w1sin[:, 0:4, :].rearrange("p t n -> p n t"))
+            elif k == 1:
+                nc.scalar.copy(out=gwb[:, :, 0], in_=w1sin[:, 4, :])
+            elif k == 2:
+                nc.scalar.copy(out=gwc[:, :, 0:3], in_=w1num[:].rearrange("p i n -> p n i"))
             else:
-                nc.vector.tensor_copy(out=ga[:], in_=planes[:].rearrange("p t b -> p b t"))
+                nc.scalar.copy(out=gw2[:], in_=w2raw[:].rearrange("p t n -> p n t"))
 
-            a_t = work.tile([P, 3, F], F32, tag="a")
+        def weight_quantise(k):
+            if k < 3:
+                gw = (gwa, gwb, gwc)[k]
+                nc.vector.quantize_mx(out=w1c[:, k, :].bitcast(FP8X4), scales=w1s[:, k, :],
+                                      in_=gw[:].rearrange("p n t -> p (n t)"))
+            else:
+                nc.vector.quantize_mx(out=w2c[:].bitcast(FP8X4), scales=w2s[:],
+                                      in_=gw2[:].rearrange("p n t -> p (n t)"))
+
+        def number_params():
+            cols_ps = ps2.tile([P, P], BF16, tag="l2", name="cols_ps")
+            nc.tensor.transpose(cols_ps[:], rows[:], ident[:])
+            nc.vector.tensor_copy(out=prm[:, 0:10], in_=cols_ps[:, 0:10])
+
+        n_t = {}
+        f_t = {}
+        planes_t = {}
+        ga_t = {}
+        a_t = {}
+        fc_t = {}
+        fs_t = {}
+        acc_t = {}
+        apl_t = {}
+        hg_t = {}
+        hc_t = {}
+        hs_t = {}
+        acc2_t = {}
+        o1_t = {}
+
+        def xview(c):
+            return xy_t[c][:].rearrange("p (b c) -> p b c", c=2)[:, :, 0]
+
+        def v_int(c, s):
+            n_t[s] = work.tile([P, F], I32, tag="n", name="n")
+            nc.vector.tensor_scalar(out=n_t[s][:], in0=xview(c), scalar1=wt[:, s:s + 1], scalar2=bt[:, s:s + 1],
+                                    op0=ALU.mult, op1=ALU.add)
+
+        def v_frac(c, s):
+            f_t[s] = work.tile([P, F], F32, tag="f", bufs=3, name="f")
+            nc.vector.scalar_tensor_tensor(out=f_t[s][:], in0=xview(c), scalar=wt[:, s:s + 1], in1=n_t[s][:],
+                                           op0=ALU.mult, op1=ALU.subtract)
+
+        def s_sin(c, s):
+            if s == 0:
+                planes_t[c] = work.tile([P, 4, F], BF16, tag="planes", name="planes")
+            dst = planes_t[c][:, s, :] if s < 4 else gb[:, :, 0]
+            nc.scalar.activation(out=dst, in_=f_t[s][:], func=ACT.Sin, bias=beta[:, s:s + 1], scale=TWO_PI)
+
+        def s_regroup(c):
+            ga_t[c] = work.tile([P, F, 4], BF16, tag="ga", align_bytes=64, name="ga")
+            nc.scalar.copy(out=ga_t[c][:], in_=planes_t[c][:].rearrange("p t b -> p b t"))
+
+        def s_affine(c):
+            a_t[c] = work.tile([P, 3, F], F32, tag="a", bufs=1, name="a")
             for i in range(3):
-                if NUM_AFFINE_ON_SCALAR:
-                    nc.scalar.activation(out=a_t[:, i, :], in_=tin[:, i, :], func=ACT.Identity,
-                                         bias=prm[:, 3 + i:4 + i], scale=prm[:, i:i + 1])
-                else:
-                    nc.vector.tensor_scalar(out=a_t[:, i, :], in0=tin[:, i, :], scalar1=prm[:, i:i + 1],
-                                            scalar2=prm[:, 3 + i:4 + i], op0=ALU.mult, op1=ALU.add)
-            a_v = a_t[:].rearrange("p i b -> p b i")
+                nc.scalar.activation(out=a_t[c][:, i, :], in_=tin_t[c][:, i, :], func=ACT.Identity,
+                                     bias=prm[:, 3 + i:4 + i], scale=prm[:, i:i + 1])
+
+        def v_number(c):
+            a_v = a_t[c][:].rearrange("p i b -> p b i")
             nc.vector.scalar_tensor_tensor(out=gc[:, :, 0:3], in0=a_v, scalar=0.01, in1=a_v,
                                            op0=ALU.mult, op1=ALU.max)
 
-            fcs = []
-            fss = []
-            for q, g in enumerate((ga, gb, gc)):
-                fc = codes.tile([P, F], U32, name="fc%d" % q, align_bytes=64)
-                fs = codes.tile([P, F], U8, name="fs%d" % q, align_bytes=64)
-                nc.vector.quantize_mx(out=fc[:].bitcast(FP8X4), scales=fs[:], in_=g[:].rearrange("p b t -> p (b t)"))
-                fcs.append(fc)
-                fss.append(fs)
+        def v_quantise(c, q):
+            g = (ga_t[c], gb, gc)[q]
+            fc_t[(c, q)] = codes.tile([P, F], U32, name="fc%d" % q, align_bytes=64)
+            fs_t[(c, q)] = codes.tile([P, F], U8, name="fs%d" % q, align_bytes=64)
+            nc.vector.quantize_mx(out=fc_t[(c, q)][:].bitcast(FP8X4), scales=fs_t[(c, q)][:],
+                                  in_=g[:].rearrange("p b t -> p (b t)"))
 
-            for half in range(F // NT):
-                j = c * (F // NT) + half
-                cs = slice(NT * half, NT * half + NT)
-                apl = hid.tile([P, 4, NT], F32, tag="apl")
+        def layer1(j, t):
+            c = j // 2
+            cs = slice(NT * (j % 2), NT * (j % 2) + NT)
+            ms = slice(P * t, P * t + P)
+            acc = ps1.tile([P, NT], F32, tag="l1", name="acc")
+            for q in range(3):
+                nc.tensor.matmul_mx(out=acc[:], lhsT=w1c[:, q, ms].bitcast(FP8X4), lhsT_scale=w1s[:, q, ms],
+                                    rhs=fc_t[(c, q)][:, cs].bitcast(FP8X4), rhs_scale=fs_t[(c, q)][:, cs],
+                                    start=(q == 0), stop=(q == 2))
+            if t == 0:
+                apl_t[j] = hid.tile([P, 4, NT], F32, tag="apl", name="apl")
+            nc.scalar.activation(out=apl_t[j][:, t, :], in_=acc[:], func=ACT.Identity,
+                                 bias=prm[:, 6 + t:7 + t], scale=1.0)
+
+        def v_hidden(j):
+            hg_t[j] = hid.tile([P, NT, 4], BF16, tag="hg", align_bytes=64, name="hg")
+            apv = apl_t[j][:].rearrange("p t b -> p b t")
+            nc.vector.scalar_tensor_tensor(out=hg_t[j][:], in0=apv, scalar=0.01, in1=apv, op0=ALU.mult, op1=ALU.max)
+
+        def v_quantise_hidden(j):
+            hc_t[j] = hid.tile([P, NT], U32, tag="hc", align_bytes=64, name="hc")
+            hs_t[j] = hid.tile([P, NT], U8, tag="hs", align_bytes=64, name="hs")
+            nc.vector.quantize_mx(out=hc_t[j][:].bitcast(FP8X4), scales=hs_t[j][:],
+                                  in_=hg_t[j][:].rearrange("p b t -> p (b t)"))
+
+        def layer2(j):
+            for i in range(4):
+                ms = slice(P * i, P * i + P)
+                acc2_t[(j, i)] = ps2.tile([P, H], F32, tag="l2", name="acc2")
+                nc.tensor.matmul_mx(out=acc2_t[(j, i)][:], lhsT=hc_t[j][:, ms].bitcast(FP8X4), lhsT_scale=hs_t[j][:, ms],
+                                    rhs=w2c[:].bitcast(FP8X4), rhs_scale=w2s[:], start=True, stop=True)
+
+        def v_bias2(j, i):
+            if i == 0:
+                o1_t[j] = outp.tile([P, 4, H], F32, tag="o1", name="o1")
+            nc.vector.tensor_tensor(out=o1_t[j][:, i, :], in0=acc2_t[(j, i)][:], in1=b2bc[:], op=ALU.add)
+
+        def v_out(j, i0, i1):
+            o = o1_t[j][:, i0:i1, :]
+            nc.vector.scalar_tensor_tensor(out=o, in0=o, scalar=0.01, in1=o, op0=ALU.mult, op1=ALU.max)
+            lo = NT * j + P * i0
+            hi = NT * j + P * i1
+            nc.sync.dma_start(out=out[lo:hi, :].rearrange("(i p) n -> p i n", p=P), in_=o)
+
+        for c in range(NCH + 1):
+            feat = c < NCH
+            back = c >= 1
+            j0 = 2 * (c - 1)
+            j1 = j0 + 1
+            if c + 1 < NCH:
+                load_xy(c + 1)
+                load_tin(c + 1)
+            if feat:
+                v_int(c, 0)
+                v_int(c, 1)
+            if c == 0:
+                weight_regroup(0)
+                weight_regroup(1)
+            if back:
+                layer1(j0, 0)
+                layer1(j0, 1)
+            if feat:
+                v_frac(c, 0)
+                s_sin(c, 0)
+                v_int(c, 2)
+            if c == 0:
+                weight_regroup(2)
+                number_params()
+            if back:
+                layer1(j0, 2)
+                layer1(j0, 3)
+            if feat:
+                v_frac(c, 1)
+                s_sin(c, 1)
+                v_int(c, 3)
+            if c == 0:
+                weight_regroup(3)
+                weight_quantise(0)
+            if back:
+                v_hidden(j0)
                 for t in range(4):
-                    acc = ps1.tile([P, NT], F32, tag="l1")
-                    ms = slice(P * t, P * t + P)
-                    for q in range(3):
-                        nc.tensor.matmul_mx(out=acc[:], lhsT=w1c[:, q, ms].bitcast(FP8X4), lhsT_scale=w1s[:, q, ms],
-                                            rhs=fcs[q][:, cs].bitcast(FP8X4), rhs_scale=fss[q][:, cs],
-                                            start=(q == 0), stop=(q == 2))
-                    nc.scalar.activation(out=apl[:, t, :], in_=acc[:], func=ACT.Identity,
-                                         bias=prm[:, 6 + t:7 + t], scale=1.0)
-                hg = hid.tile([P, NT, 4], BF16, tag="hg", align_bytes=64)
-                apv = apl[:].rearrange("p t b -> p b t")
-                nc.vector.scalar_tensor_tensor(out=hg[:], in0=apv, scalar=0.01, in1=apv, op0=ALU.mult, op1=ALU.max)
-                hc = hid.tile([P, NT], U32, tag="hc", align_bytes=64)
-                hs = hid.tile([P, NT], U8, tag="hs", align_bytes=64)
-                nc.vector.quantize_mx(out=hc[:].bitcast(FP8X4), scales=hs[:], in_=hg[:].rearrange("p b t -> p (b t)"))
-                o1 = outp.tile([P, 4, H], F32, tag="o1")
+                    layer1(j1, t)
+            if feat:
+                v_frac(c, 2)
+                s_sin(c, 2)
+            if c == 0:
+                weight_quantise(1)
+            if back:
+                v_quantise_hidden(j0)
+                layer2(j0)
+            if feat:
+                v_int(c, 4)
+                v_frac(c, 3)
+                s_sin(c, 3)
+                s_affine(c)
+                s_regroup(c)
+            if c == 0:
+                weight_quantise(2)
+            if back and feat:
                 for i in range(4):
-                    acc2 = ps2.tile([P, H], F32, tag="l2")
-                    ms = slice(P * i, P * i + P)
-                    nc.tensor.matmul_mx(out=acc2[:], lhsT=hc[:, ms].bitcast(FP8X4), lhsT_scale=hs[:, ms],
-                                        rhs=w2c[:].bitcast(FP8X4), rhs_scale=w2s[:], start=True, stop=True)
-                    nc.vector.tensor_tensor(out=o1[:, i, :], in0=acc2[:], in1=b2bc[:], op=ALU.add)
-                nc.vector.scalar_tensor_tensor(out=o1[:], in0=o1[:], scalar=0.01, in1=o1[:], op0=ALU.mult, op1=ALU.max)
-                nc.sync.dma_start(out=out[NT * j:NT * j + NT, :].rearrange("(i p) n -> p i n", p=P), in_=o1[:])
+                    v_bias2(j0, i)
+                v_hidden(j1)
+                v_out(j0, 0, 4)
+                v_quantise_hidden(j1)
+                layer2(j1)
+            if feat:
+                v_frac(c, 4)
+                s_sin(c, 4)
+            if c == 0:
+                weight_quantise(3)
+            if feat:
+                v_number(c)
+            if back and feat:
+                for i in range(4):
+                    v_bias2(j1, i)
+            if feat:
+                v_quantise(c, 2)
+                v_quantise(c, 1)
+                v_quantise(c, 0)
+            if back and feat:
+                v_out(j1, 0, 4)
+            if not feat:
+                v_hidden(j1)
+                for i in range(4):
+                    v_bias2(j0, i)
+                v_quantise_hidden(j1)
+                layer2(j1)
+                v_out(j0, 0, 4)
+                v_bias2(j1, 0)
+                v_bias2(j1, 1)
+                v_out(j1, 0, 1)
+                v_bias2(j1, 2)
+                v_out(j1, 1, 2)
+                v_bias2(j1, 3)
+                v_out(j1, 2, 3)
+                v_out(j1, 3, 4)

@@ -34,10 +34,10 @@ def tile_claimencoder_t_kernel(
     with ExitStack() as ctx:
         ctx.enter_context(tc.manual_schedule())
         const = ctx.enter_context(tc.tile_pool(name="const", bufs=1))
-        ps1 = ctx.enter_context(tc.psum_pool(name="ps1", bufs=4))
-        ps2 = ctx.enter_context(tc.psum_pool(name="ps2", bufs=4))
-        stage = ctx.enter_context(tc.tile_pool(name="stage", bufs=1))
-        outp = ctx.enter_context(tc.tile_pool(name="outp", bufs=3))
+        ps1 = ctx.enter_context(tc.psum_pool(name="ps1", bufs=3))
+        ps2 = ctx.enter_context(tc.psum_pool(name="ps2", bufs=2))
+        ps3 = ctx.enter_context(tc.psum_pool(name="ps3", bufs=3))
+        big = ctx.enter_context(tc.tile_pool(name="big", bufs=2))
         hid = ctx.enter_context(tc.tile_pool(name="hid", bufs=2))
         inp = ctx.enter_context(tc.tile_pool(name="inp", bufs=2))
         work = ctx.enter_context(tc.tile_pool(name="work", bufs=2))
@@ -64,12 +64,14 @@ def tile_claimencoder_t_kernel(
 
         ident = const.tile([P, P], BF16)
         make_identity(nc, ident[:])
-        w1sin = stage.tile([P, 5, H], BF16)
+        w1sin = big.tile([P, 5, H], BF16, tag="ot", align_bytes=64)
         nc.gpsimd.dma_start(out=w1sin[:], in_=W1[0:640, :].rearrange("(p s) n -> p s n", s=5))
-        w1num = stage.tile([P, 3, H], BF16)
+        w1num = big.tile([P, 3, H], BF16, tag="ot", align_bytes=64)
         nc.gpsimd.dma_start(out=w1num[:], in_=W1[640:1024, :].rearrange("(i p) n -> p i n", p=P))
-        w2raw = stage.tile([P, 4, H], BF16)
+        w2raw = big.tile([P, 4, H], BF16, tag="o", bufs=3, align_bytes=64)
         nc.gpsimd.dma_start(out=w2raw[:], in_=W2.rearrange("(t p) n -> p t n", p=P))
+        ident32 = const.tile([P, P], F32)
+        make_identity(nc, ident32[:])
 
         wsin = const.tile([P, 5], BF16)
         bsin = const.tile([P, 5], BF16)
@@ -88,11 +90,10 @@ def tile_claimencoder_t_kernel(
         for i, v in enumerate((t_w, ws_w, wd_w, t_b, ws_b, wd_b)):
             nc.scalar.dma_start(out=rows[i:i + 1, :], in_=v.rearrange("(o n) -> o n", o=1))
         nc.scalar.dma_start(out=rows[6:10, :], in_=b1.rearrange("(t p) -> t p", p=P))
+        nc.scalar.dma_start(out=rows[10:14, :], in_=b2.rearrange("(t p) -> t p", p=P))
         load_tin(0)
-        b2bc = const.tile([P, H], BF16)
-        nc.sync.dma_start(out=b2bc[:], in_=b2.partition_broadcast(P))
 
-        mark_ps = ps2.tile([P, P], BF16, tag="l2")
+        mark_ps = ps3.tile([P, P], BF16, tag="tb")
         nc.tensor.transpose(mark_ps[:], mark[:], ident[:])
         is_cos = const.tile([P, 1], F32)
         nc.vector.tensor_copy(out=is_cos[:], in_=mark_ps[:, 0:1])
@@ -105,10 +106,10 @@ def tile_claimencoder_t_kernel(
         nc.vector.memset(gb[:], 0.0)
         gc = const.tile([P, F, 4], BF16, align_bytes=64)
         nc.vector.memset(gc[:], 0.0)
-        gwa = stage.tile([P, H, 4], BF16, align_bytes=64)
-        gwb = stage.tile([P, H, 4], BF16, align_bytes=64)
-        gwc = stage.tile([P, H, 4], BF16, align_bytes=64)
-        gw2 = stage.tile([P, H, 4], BF16, align_bytes=64)
+        gwa = big.tile([P, H, 4], BF16, tag="o", bufs=3, align_bytes=64)
+        gwb = big.tile([P, H, 4], BF16, tag="o", bufs=3, align_bytes=64)
+        gwc = big.tile([P, H, 4], BF16, tag="apl", align_bytes=64)
+        gw2 = big.tile([P, H, 4], BF16, tag="apl", align_bytes=64)
         nc.vector.memset(gwb[:], 0.0)
         nc.vector.memset(gwc[:], 0.0)
 
@@ -145,9 +146,9 @@ def tile_claimencoder_t_kernel(
                                       in_=gw2[:].rearrange("p n t -> p (n t)"))
 
         def number_params():
-            cols_ps = ps2.tile([P, P], BF16, tag="l2", name="cols_ps")
+            cols_ps = ps3.tile([P, P], BF16, tag="tb", name="cols_ps")
             nc.tensor.transpose(cols_ps[:], rows[:], ident[:])
-            nc.vector.tensor_copy(out=prm[:, 0:10], in_=cols_ps[:, 0:10])
+            nc.vector.tensor_copy(out=prm[:, 0:14], in_=cols_ps[:, 0:14])
 
         n_t = {}
         f_t = {}
@@ -156,13 +157,12 @@ def tile_claimencoder_t_kernel(
         a_t = {}
         fc_t = {}
         fs_t = {}
-        acc_t = {}
         apl_t = {}
         hg_t = {}
         hc_t = {}
         hs_t = {}
-        acc2_t = {}
-        o1_t = {}
+        ot_t = {}
+        o_t = {}
 
         def xview(c):
             return xy_t[c][:].rearrange("p (b c) -> p b c", c=2)[:, :, 0]
@@ -187,11 +187,11 @@ def tile_claimencoder_t_kernel(
             ga_t[c] = work.tile([P, F, 4], BF16, tag="ga", align_bytes=64, name="ga")
             nc.scalar.copy(out=ga_t[c][:], in_=planes_t[c][:].rearrange("p t b -> p b t"))
 
-        def s_affine(c):
+        def v_affine(c):
             a_t[c] = work.tile([P, 3, F], F32, tag="a", bufs=1, name="a")
             for i in range(3):
-                nc.scalar.activation(out=a_t[c][:, i, :], in_=tin_t[c][:, i, :], func=ACT.Identity,
-                                     bias=prm[:, 3 + i:4 + i], scale=prm[:, i:i + 1])
+                nc.vector.tensor_scalar(out=a_t[c][:, i, :], in0=tin_t[c][:, i, :], scalar1=prm[:, i:i + 1],
+                                        scalar2=prm[:, 3 + i:4 + i], op0=ALU.mult, op1=ALU.add)
 
         def v_number(c):
             a_v = a_t[c][:].rearrange("p i b -> p b i")
@@ -205,19 +205,19 @@ def tile_claimencoder_t_kernel(
             nc.vector.quantize_mx(out=fc_t[(c, q)][:].bitcast(FP8X4), scales=fs_t[(c, q)][:],
                                   in_=g[:].rearrange("p b t -> p (b t)"))
 
-        def layer1(j, t):
+        def layer1(j):
             c = j // 2
             cs = slice(NT * (j % 2), NT * (j % 2) + NT)
-            ms = slice(P * t, P * t + P)
-            acc = ps1.tile([P, NT], F32, tag="l1", name="acc")
-            for q in range(3):
-                nc.tensor.matmul_mx(out=acc[:], lhsT=w1c[:, q, ms].bitcast(FP8X4), lhsT_scale=w1s[:, q, ms],
-                                    rhs=fc_t[(c, q)][:, cs].bitcast(FP8X4), rhs_scale=fs_t[(c, q)][:, cs],
-                                    start=(q == 0), stop=(q == 2))
-            if t == 0:
-                apl_t[j] = hid.tile([P, 4, NT], F32, tag="apl", name="apl")
-            nc.scalar.activation(out=apl_t[j][:, t, :], in_=acc[:], func=ACT.Identity,
-                                 bias=prm[:, 6 + t:7 + t], scale=1.0)
+            apl_t[j] = big.tile([P, 4, NT], F32, tag="apl", name="apl", align_bytes=64)
+            for t in range(4):
+                ms = slice(P * t, P * t + P)
+                acc = ps1.tile([P, NT], F32, tag="l1", name="acc")
+                for q in range(3):
+                    nc.tensor.matmul_mx(out=acc[:], lhsT=w1c[:, q, ms].bitcast(FP8X4), lhsT_scale=w1s[:, q, ms],
+                                        rhs=fc_t[(c, q)][:, cs].bitcast(FP8X4), rhs_scale=fs_t[(c, q)][:, cs],
+                                        start=(q == 0), stop=(q == 2))
+                nc.scalar.activation(out=apl_t[j][:, t, :], in_=acc[:], func=ACT.Identity,
+                                     bias=prm[:, 6 + t:7 + t], scale=1.0)
 
         def v_hidden(j):
             hg_t[j] = hid.tile([P, NT, 4], BF16, tag="hg", align_bytes=64, name="hg")
@@ -231,23 +231,30 @@ def tile_claimencoder_t_kernel(
                                   in_=hg_t[j][:].rearrange("p b t -> p (b t)"))
 
         def layer2(j):
-            for i in range(4):
-                ms = slice(P * i, P * i + P)
-                acc2_t[(j, i)] = ps2.tile([P, H], F32, tag="l2", name="acc2")
-                nc.tensor.matmul_mx(out=acc2_t[(j, i)][:], lhsT=hc_t[j][:, ms].bitcast(FP8X4), lhsT_scale=hs_t[j][:, ms],
-                                    rhs=w2c[:].bitcast(FP8X4), rhs_scale=w2s[:], start=True, stop=True)
+            ot_t[j] = big.tile([P, 4, NT], F32, tag="ot", name="ot", align_bytes=64)
+            for m in range(4):
+                ms = slice(P * m, P * m + P)
+                acc2 = ps2.tile([P, NT], F32, tag="l2", name="acc2")
+                nc.tensor.matmul_mx(out=acc2[:], lhsT=w2c[:, ms].bitcast(FP8X4), lhsT_scale=w2s[:, ms],
+                                    rhs=hc_t[j][:].bitcast(FP8X4), rhs_scale=hs_t[j][:], start=True, stop=True)
+                nc.scalar.activation(out=ot_t[j][:, m, :], in_=acc2[:], func=ACT.Identity,
+                                     bias=prm[:, 10 + m:11 + m], scale=1.0)
 
-        def v_bias2(j, i):
-            if i == 0:
-                o1_t[j] = outp.tile([P, 4, H], F32, tag="o1", name="o1")
-            nc.vector.tensor_tensor(out=o1_t[j][:, i, :], in0=acc2_t[(j, i)][:], in1=b2bc[:], op=ALU.add)
-
-        def v_out(j, i0, i1):
-            o = o1_t[j][:, i0:i1, :]
+        def v_lrelu(j, i0, i1):
+            o = ot_t[j][:, :, P * i0:P * i1]
             nc.vector.scalar_tensor_tensor(out=o, in0=o, scalar=0.01, in1=o, op0=ALU.mult, op1=ALU.max)
+
+        def turn(j, i0, i1):
+            if i0 == 0:
+                o_t[j] = big.tile([P, 4, H], F32, tag="o", bufs=3, name="o", align_bytes=64)
+            for i in range(i0, i1):
+                tb = ps3.tile([P, H], F32, tag="tb", name="tb")
+                for m in range(4):
+                    nc.tensor.transpose(tb[:, P * m:P * m + P], ot_t[j][:, m, P * i:P * i + P], ident32[:])
+                nc.scalar.copy(out=o_t[j][:, i, :], in_=tb[:])
             lo = NT * j + P * i0
             hi = NT * j + P * i1
-            nc.sync.dma_start(out=out[lo:hi, :].rearrange("(i p) n -> p i n", p=P), in_=o)
+            nc.sync.dma_start(out=out[lo:hi, :].rearrange("(i p) n -> p i n", p=P), in_=o_t[j][:, i0:i1, :])
 
         for c in range(NCH + 1):
             feat = c < NCH
@@ -263,19 +270,17 @@ def tile_claimencoder_t_kernel(
             if c == 0:
                 weight_regroup(0)
                 weight_regroup(1)
+                number_params()
             if back:
-                layer1(j0, 0)
-                layer1(j0, 1)
+                layer1(j0)
+            if c >= 2:
+                turn(j0 - 1, 0, 4)
             if feat:
                 v_frac(c, 0)
                 s_sin(c, 0)
                 v_int(c, 2)
             if c == 0:
                 weight_regroup(2)
-                number_params()
-            if back:
-                layer1(j0, 2)
-                layer1(j0, 3)
             if feat:
                 v_frac(c, 1)
                 s_sin(c, 1)
@@ -285,8 +290,7 @@ def tile_claimencoder_t_kernel(
                 weight_quantise(0)
             if back:
                 v_hidden(j0)
-                for t in range(4):
-                    layer1(j1, t)
+                layer1(j1)
             if feat:
                 v_frac(c, 2)
                 s_sin(c, 2)
@@ -299,45 +303,34 @@ def tile_claimencoder_t_kernel(
                 v_int(c, 4)
                 v_frac(c, 3)
                 s_sin(c, 3)
-                s_affine(c)
-                s_regroup(c)
             if c == 0:
                 weight_quantise(2)
-            if back and feat:
-                for i in range(4):
-                    v_bias2(j0, i)
+            if back:
                 v_hidden(j1)
-                v_out(j0, 0, 4)
-                v_quantise_hidden(j1)
-                layer2(j1)
             if feat:
+                s_regroup(c)
                 v_frac(c, 4)
-                s_sin(c, 4)
             if c == 0:
                 weight_quantise(3)
+            if back:
+                v_quantise_hidden(j1)
+            if feat:
+                v_affine(c)
+            if back:
+                v_lrelu(j0, 0, 4)
+            if feat:
+                s_sin(c, 4)
+            if back:
+                layer2(j1)
+                turn(j0, 0, 4)
             if feat:
                 v_number(c)
-            if back and feat:
-                for i in range(4):
-                    v_bias2(j1, i)
-            if feat:
-                v_quantise(c, 2)
                 v_quantise(c, 1)
+                v_quantise(c, 2)
                 v_quantise(c, 0)
             if back and feat:
-                v_out(j1, 0, 4)
-            if not feat:
-                v_hidden(j1)
-                for i in range(4):
-                    v_bias2(j0, i)
-                v_quantise_hidden(j1)
-                layer2(j1)
-                v_out(j0, 0, 4)
-                v_bias2(j1, 0)
-                v_bias2(j1, 1)
-                v_out(j1, 0, 1)
-                v_bias2(j1, 2)
-                v_out(j1, 1, 2)
-                v_bias2(j1, 3)
-                v_out(j1, 2, 3)
-                v_out(j1, 3, 4)
+                v_lrelu(j1, 0, 4)
+        last = 2 * NCH - 1
+        for i in range(4):
+            v_lrelu(last, i, i + 1)
+            turn(last, i, i + 1)

@@ -34,9 +34,7 @@ def tile_claimencoder_t_kernel(
     with ExitStack() as ctx:
         ctx.enter_context(tc.manual_schedule())
         const = ctx.enter_context(tc.tile_pool(name="const", bufs=1))
-        ps1 = ctx.enter_context(tc.psum_pool(name="ps1", bufs=3))
-        ps2 = ctx.enter_context(tc.psum_pool(name="ps2", bufs=2))
-        ps3 = ctx.enter_context(tc.psum_pool(name="ps3", bufs=3))
+        psum = ctx.enter_context(tc.psum_pool(name="psum", bufs=8))
         big = ctx.enter_context(tc.tile_pool(name="big", bufs=2))
         hid = ctx.enter_context(tc.tile_pool(name="hid", bufs=2))
         inp = ctx.enter_context(tc.tile_pool(name="inp", bufs=2))
@@ -93,7 +91,7 @@ def tile_claimencoder_t_kernel(
         nc.scalar.dma_start(out=rows[10:14, :], in_=b2.rearrange("(t p) -> t p", p=P))
         load_tin(0)
 
-        mark_ps = ps3.tile([P, P], BF16, tag="tb")
+        mark_ps = psum.tile([P, P], BF16, tag="bank")
         nc.tensor.transpose(mark_ps[:], mark[:], ident[:])
         is_cos = const.tile([P, 1], F32)
         nc.vector.tensor_copy(out=is_cos[:], in_=mark_ps[:, 0:1])
@@ -110,8 +108,8 @@ def tile_claimencoder_t_kernel(
         gwb = big.tile([P, H, 4], BF16, tag="o", bufs=3, align_bytes=64)
         gwc = big.tile([P, H, 4], BF16, tag="apl", align_bytes=64)
         gw2 = big.tile([P, H, 4], BF16, tag="apl", align_bytes=64)
-        nc.vector.memset(gwb[:], 0.0)
-        nc.vector.memset(gwc[:], 0.0)
+        nc.gpsimd.memset(gwb[:], 0.0)
+        nc.gpsimd.memset(gwc[:], 0.0)
 
         wt = const.tile([P, 5], F32)
         nc.vector.tensor_scalar(out=wt[:], in0=wsin[:], scalar1=1.0 / TWO_PI, scalar2=None, op0=ALU.mult)
@@ -146,7 +144,7 @@ def tile_claimencoder_t_kernel(
                                       in_=gw2[:].rearrange("p n t -> p (n t)"))
 
         def number_params():
-            cols_ps = ps3.tile([P, P], BF16, tag="tb", name="cols_ps")
+            cols_ps = psum.tile([P, P], BF16, tag="bank", name="cols_ps")
             nc.tensor.transpose(cols_ps[:], rows[:], ident[:])
             nc.vector.tensor_copy(out=prm[:, 0:14], in_=cols_ps[:, 0:14])
 
@@ -185,7 +183,8 @@ def tile_claimencoder_t_kernel(
 
         def s_regroup(c):
             ga_t[c] = work.tile([P, F, 4], BF16, tag="ga", align_bytes=64, name="ga")
-            nc.scalar.copy(out=ga_t[c][:], in_=planes_t[c][:].rearrange("p t b -> p b t"))
+            nc.scalar.copy(out=ga_t[c][:].rearrange("p (c i) t -> p c t i", i=4),
+                           in_=planes_t[c][:].rearrange("p t (c i) -> p c t i", i=4))
 
         def v_affine(c):
             a_t[c] = work.tile([P, 3, F], F32, tag="a", bufs=1, name="a")
@@ -211,7 +210,7 @@ def tile_claimencoder_t_kernel(
             apl_t[j] = big.tile([P, 4, NT], F32, tag="apl", name="apl", align_bytes=64)
             for t in range(4):
                 ms = slice(P * t, P * t + P)
-                acc = ps1.tile([P, NT], F32, tag="l1", name="acc")
+                acc = psum.tile([P, NT], F32, tag="bank", name="acc")
                 for q in range(3):
                     nc.tensor.matmul_mx(out=acc[:], lhsT=w1c[:, q, ms].bitcast(FP8X4), lhsT_scale=w1s[:, q, ms],
                                         rhs=fc_t[(c, q)][:, cs].bitcast(FP8X4), rhs_scale=fs_t[(c, q)][:, cs],
@@ -234,7 +233,7 @@ def tile_claimencoder_t_kernel(
             ot_t[j] = big.tile([P, 4, NT], F32, tag="ot", name="ot", align_bytes=64)
             for m in range(4):
                 ms = slice(P * m, P * m + P)
-                acc2 = ps2.tile([P, NT], F32, tag="l2", name="acc2")
+                acc2 = psum.tile([P, NT], F32, tag="bank", name="acc2")
                 nc.tensor.matmul_mx(out=acc2[:], lhsT=w2c[:, ms].bitcast(FP8X4), lhsT_scale=w2s[:, ms],
                                     rhs=hc_t[j][:].bitcast(FP8X4), rhs_scale=hs_t[j][:], start=True, stop=True)
                 nc.scalar.activation(out=ot_t[j][:, m, :], in_=acc2[:], func=ACT.Identity,
@@ -248,7 +247,7 @@ def tile_claimencoder_t_kernel(
             if i0 == 0:
                 o_t[j] = big.tile([P, 4, H], F32, tag="o", bufs=3, name="o", align_bytes=64)
             for i in range(i0, i1):
-                tb = ps3.tile([P, H], F32, tag="tb", name="tb")
+                tb = psum.tile([P, H], F32, tag="bank", name="tb")
                 for m in range(4):
                     nc.tensor.transpose(tb[:, P * m:P * m + P], ot_t[j][:, m, P * i:P * i + P], ident32[:])
                 nc.scalar.copy(out=o_t[j][:, i, :], in_=tb[:])
@@ -273,8 +272,6 @@ def tile_claimencoder_t_kernel(
                 number_params()
             if back:
                 layer1(j0)
-            if c >= 2:
-                turn(j0 - 1, 0, 4)
             if feat:
                 v_frac(c, 0)
                 s_sin(c, 0)
@@ -289,7 +286,6 @@ def tile_claimencoder_t_kernel(
                 weight_regroup(3)
                 weight_quantise(0)
             if back:
-                v_hidden(j0)
                 layer1(j1)
             if feat:
                 v_frac(c, 2)
@@ -297,8 +293,9 @@ def tile_claimencoder_t_kernel(
             if c == 0:
                 weight_quantise(1)
             if back:
-                v_quantise_hidden(j0)
-                layer2(j0)
+                v_hidden(j0)
+            if c >= 2:
+                turn(j0 - 1, 0, 4)
             if feat:
                 v_int(c, 4)
                 v_frac(c, 3)
@@ -306,25 +303,25 @@ def tile_claimencoder_t_kernel(
             if c == 0:
                 weight_quantise(2)
             if back:
-                v_hidden(j1)
+                v_quantise_hidden(j0)
+                layer2(j0)
             if feat:
-                s_regroup(c)
                 v_frac(c, 4)
+                s_sin(c, 4)
+                v_affine(c)
             if c == 0:
                 weight_quantise(3)
             if back:
+                v_hidden(j1)
+            if feat:
+                s_regroup(c)
+                v_number(c)
+            if back:
                 v_quantise_hidden(j1)
-            if feat:
-                v_affine(c)
-            if back:
-                v_lrelu(j0, 0, 4)
-            if feat:
-                s_sin(c, 4)
-            if back:
                 layer2(j1)
+                v_lrelu(j0, 0, 4)
                 turn(j0, 0, 4)
             if feat:
-                v_number(c)
                 v_quantise(c, 1)
                 v_quantise(c, 2)
                 v_quantise(c, 0)

@@ -243,14 +243,26 @@ def tile_claimencoder_t_kernel(
             o = ot_t[j][:, :, P * i0:P * i1]
             nc.vector.scalar_tensor_tensor(out=o, in0=o, scalar=0.01, in1=o, op0=ALU.mult, op1=ALU.max)
 
-        def turn(j, i0, i1):
+        tb_t = {}
+
+        def turn(j, i0, i1, on_vector=0):
             if i0 == 0:
                 o_t[j] = big.tile([P, 4, H], F32, tag="o", bufs=3, name="o", align_bytes=64)
             for i in range(i0, i1):
                 tb = psum.tile([P, H], F32, tag="bank", name="tb")
                 for m in range(4):
                     nc.tensor.transpose(tb[:, P * m:P * m + P], ot_t[j][:, m, P * i:P * i + P], ident32[:])
-                nc.scalar.copy(out=o_t[j][:, i, :], in_=tb[:])
+                if i < i1 - on_vector:
+                    nc.scalar.copy(out=o_t[j][:, i, :], in_=tb[:])
+                else:
+                    tb_t[(j, i)] = tb
+            if on_vector == 0:
+                store(j, i0, i1)
+
+        def v_copy_out(j, i):
+            nc.vector.tensor_copy(out=o_t[j][:, i, :], in_=tb_t[(j, i)][:])
+
+        def store(j, i0, i1):
             lo = NT * j + P * i0
             hi = NT * j + P * i1
             nc.sync.dma_start(out=out[lo:hi, :].rearrange("(i p) n -> p i n", p=P), in_=o_t[j][:, i0:i1, :])
@@ -295,11 +307,14 @@ def tile_claimencoder_t_kernel(
             if back:
                 v_hidden(j0)
             if c >= 2:
-                turn(j0 - 1, 0, 4)
+                turn(j0 - 1, 0, 4, on_vector=1)
             if feat:
                 v_int(c, 4)
                 v_frac(c, 3)
                 s_sin(c, 3)
+            if c >= 2:
+                v_copy_out(j0 - 1, 3)
+                store(j0 - 1, 0, 4)
             if c == 0:
                 weight_quantise(2)
             if back:

@@ -186,9 +186,13 @@ def tile_claimencoder_t_kernel(
             nc.scalar.copy(out=ga_t[c][:].rearrange("p (c i) t -> p c t i", i=4),
                            in_=planes_t[c][:].rearrange("p t (c i) -> p c t i", i=4))
 
-        def v_affine(c):
+        def s_affine(c):
             a_t[c] = work.tile([P, 3, F], F32, tag="a", bufs=1, name="a")
-            for i in range(3):
+            nc.scalar.activation(out=a_t[c][:, 2, :], in_=tin_t[c][:, 2, :], func=ACT.Identity,
+                                 bias=prm[:, 5:6], scale=prm[:, 2:3])
+
+        def v_affine(c):
+            for i in range(2):
                 nc.vector.tensor_scalar(out=a_t[c][:, i, :], in0=tin_t[c][:, i, :], scalar1=prm[:, i:i + 1],
                                         scalar2=prm[:, 3 + i:4 + i], op0=ALU.mult, op1=ALU.add)
 
@@ -243,26 +247,14 @@ def tile_claimencoder_t_kernel(
             o = ot_t[j][:, :, P * i0:P * i1]
             nc.vector.scalar_tensor_tensor(out=o, in0=o, scalar=0.01, in1=o, op0=ALU.mult, op1=ALU.max)
 
-        tb_t = {}
-
-        def turn(j, i0, i1, on_vector=0):
+        def turn(j, i0, i1):
             if i0 == 0:
                 o_t[j] = big.tile([P, 4, H], F32, tag="o", bufs=3, name="o", align_bytes=64)
             for i in range(i0, i1):
                 tb = psum.tile([P, H], F32, tag="bank", name="tb")
                 for m in range(4):
                     nc.tensor.transpose(tb[:, P * m:P * m + P], ot_t[j][:, m, P * i:P * i + P], ident32[:])
-                if i < i1 - on_vector:
-                    nc.scalar.copy(out=o_t[j][:, i, :], in_=tb[:])
-                else:
-                    tb_t[(j, i)] = tb
-            if on_vector == 0:
-                store(j, i0, i1)
-
-        def v_copy_out(j, i):
-            nc.vector.tensor_copy(out=o_t[j][:, i, :], in_=tb_t[(j, i)][:])
-
-        def store(j, i0, i1):
+                nc.scalar.copy(out=o_t[j][:, i, :], in_=tb[:])
             lo = NT * j + P * i0
             hi = NT * j + P * i1
             nc.sync.dma_start(out=out[lo:hi, :].rearrange("(i p) n -> p i n", p=P), in_=o_t[j][:, i0:i1, :])
@@ -307,14 +299,12 @@ def tile_claimencoder_t_kernel(
             if back:
                 v_hidden(j0)
             if c >= 2:
-                turn(j0 - 1, 0, 4, on_vector=1)
+                turn(j0 - 1, 0, 4)
             if feat:
                 v_int(c, 4)
                 v_frac(c, 3)
                 s_sin(c, 3)
-            if c >= 2:
-                v_copy_out(j0 - 1, 3)
-                store(j0 - 1, 0, 4)
+                s_affine(c)
             if c == 0:
                 weight_quantise(2)
             if back:

import math
from contextlib import ExitStack

import concourse.mybir as mybir
from concourse.masks import make_identity

FLOPS = 2 * 6144 * (1024 * 512 + 512 * 512)

F32 = mybir.dt.float32
BF16 = mybir.dt.bfloat16
I32 = mybir.dt.int32
U32 = mybir.dt.uint32
U8 = mybir.dt.uint8
FP8X4 = mybir.dt.float8_e4m3fn_x4
ALU = mybir.AluOpType
ACT = mybir.ActivationFunctionType

P = 128
B = 6144
F = 1024
NT = 512
H = 512
NCH = B // F
TWO_PI = 2.0 * math.pi


def tile_claimencoder_t_kernel(
    tc, src_xy, dst_xy, time_s, wait_src, wait_dst,
    src_wsx, src_bsx, src_wcx, src_bcx, src_wsy, src_bsy, src_wcy, src_bcy,
    dst_wsx, dst_bsx, dst_wcx, dst_bcx, dst_wsy, dst_bsy, dst_wcy, dst_bcy,
    t_w, t_b, ws_w, ws_b, wd_w, wd_b, W1, b1, W2, b2, out,
):
    nc = tc.nc
    with ExitStack() as ctx:
        ctx.enter_context(tc.manual_schedule())
        const = ctx.enter_context(tc.tile_pool(name="const", bufs=1))
        psum = ctx.enter_context(tc.psum_pool(name="psum", bufs=8))
        big = ctx.enter_context(tc.tile_pool(name="big", bufs=2))
        hid = ctx.enter_context(tc.tile_pool(name="hid", bufs=2))
        inp = ctx.enter_context(tc.tile_pool(name="inp", bufs=2))
        work = ctx.enter_context(tc.tile_pool(name="work", bufs=2))
        codes = ctx.enter_context(tc.tile_pool(name="codes", bufs=2))

        src_flat = src_xy.rearrange("b c -> (b c)")
        dst_flat = dst_xy.rearrange("b c -> (b c)")
        xy_t = {}
        tin_t = {}

        def load_xy(c):
            xy = inp.tile([P, 2 * F], BF16, tag="xy", name="xy")
            for q, (flat, off) in enumerate(((src_flat, 0), (src_flat, 1), (dst_flat, 0), (dst_flat, 1))):
                n_el = 2 * F - off
                lo = 2 * F * c + off
                nc.sync.dma_start(out=xy[32 * q:32 * q + 32, 0:n_el], in_=flat[lo:lo + n_el].partition_broadcast(32))
            xy_t[c] = xy

        def load_tin(c):
            tin = inp.tile([P, 3, F], BF16, tag="tin", name="tin")
            for i, v in enumerate((time_s, wait_src, wait_dst)):
                nc.sync.dma_start(out=tin[:, i, :], in_=v[F * c:F * c + F].partition_broadcast(P))
            tin_t[c] = tin

        ident = const.tile([P, P], BF16)
        make_identity(nc, ident[:])
        w1sin = big.tile([P, 5, H], BF16, tag="ot", align_bytes=64)
        nc.gpsimd.dma_start(out=w1sin[:], in_=W1[0:640, :].rearrange("(p s) n -> p s n", s=5))
        w1num = big.tile([P, 3, H], BF16, tag="ot", align_bytes=64)
        nc.gpsimd.dma_start(out=w1num[:], in_=W1[640:1024, :].rearrange("(i p) n -> p i n", p=P))
        w2raw = big.tile([P, 4, H], BF16, tag="o", bufs=3, align_bytes=64)
        nc.gpsimd.dma_start(out=w2raw[:], in_=W2.rearrange("(t p) n -> p t n", p=P))
        ident32 = const.tile([P, P], F32)
        make_identity(nc, ident32[:])

        wsin = const.tile([P, 5], BF16)
        bsin = const.tile([P, 5], BF16)
        w_vecs = (src_wsx, src_wcx, src_wsy, src_wcy, dst_wsx, dst_wcx, dst_wsy, dst_wcy)
        b_vecs = (src_bsx, src_bcx, src_bsy, src_bcy, dst_bsx, dst_bcx, dst_bsy, dst_bcy)
        for g in range(8):
            nc.sync.dma_start(out=wsin[16 * g:16 * g + 16, :], in_=w_vecs[g].rearrange("(r s) -> r s", s=5))
            nc.scalar.dma_start(out=bsin[16 * g:16 * g + 16, :], in_=b_vecs[g].rearrange("(r s) -> r s", s=5))
        load_xy(0)

        mark = const.tile([P, P], BF16)
        nc.vector.memset(mark[:], 0.0)
        nc.vector.memset(mark[0:1, :].rearrange("o (g h r) -> o g h r", h=2, r=16)[:, :, 1, :], 1.0)
        rows = const.tile([P, P], BF16)
        nc.vector.memset(rows[:], 0.0)
        for i, v in enumerate((t_w, ws_w, wd_w, t_b, ws_b, wd_b)):
            nc.scalar.dma_start(out=rows[i:i + 1, :], in_=v.rearrange("(o n) -> o n", o=1))
        nc.scalar.dma_start(out=rows[6:10, :], in_=b1.rearrange("(t p) -> t p", p=P))
        nc.scalar.dma_start(out=rows[10:14, :], in_=b2.rearrange("(t p) -> t p", p=P))
        load_tin(0)

        mark_ps = psum.tile([P, P], BF16, tag="bank")
        nc.tensor.transpose(mark_ps[:], mark[:], ident[:])
        is_cos = const.tile([P, 1], F32)
        nc.vector.tensor_copy(out=is_cos[:], in_=mark_ps[:, 0:1])
        quarter = const.tile([P, 1], F32)
        nc.vector.tensor_scalar(out=quarter[:], in0=is_cos[:], scalar1=0.25, scalar2=None, op0=ALU.mult)
        halfpi = const.tile([P, 1], F32)
        nc.vector.tensor_scalar(out=halfpi[:], in0=is_cos[:], scalar1=0.5 * math.pi, scalar2=None, op0=ALU.mult)

        gb = const.tile([P, F, 4], BF16, align_bytes=64)
        nc.vector.memset(gb[:], 0.0)
        gc = const.tile([P, F, 4], BF16, align_bytes=64)
        nc.vector.memset(gc[:], 0.0)
        gwa = big.tile([P, H, 4], BF16, tag="o", bufs=3, align_bytes=64)
        gwb = big.tile([P, H, 4], BF16, tag="o", bufs=3, align_bytes=64)
        gwc = big.tile([P, H, 4], BF16, tag="apl", align_bytes=64)
        gw2 = big.tile([P, H, 4], BF16, tag="apl", align_bytes=64)
        nc.gpsimd.memset(gwb[:], 0.0)
        nc.gpsimd.memset(gwc[:], 0.0)

        wt = const.tile([P, 5], F32)
        nc.vector.tensor_scalar(out=wt[:], in0=wsin[:], scalar1=1.0 / TWO_PI, scalar2=None, op0=ALU.mult)
        bt = const.tile([P, 5], F32)
        nc.vector.tensor_scalar(out=bt[:], in0=bsin[:], scalar1=1.0 / TWO_PI, scalar2=quarter[:, 0:1], op0=ALU.mult, op1=ALU.add)
        beta = const.tile([P, 5], F32)
        nc.vector.tensor_scalar(out=beta[:], in0=bsin[:], scalar1=halfpi[:, 0:1], scalar2=None, op0=ALU.add)

        w1c = const.tile([P, 3, H], U32, align_bytes=64)
        w1s = const.tile([P, 3, H], U8, align_bytes=64)
        w2c = const.tile([P, H], U32, align_bytes=64)
        w2s = const.tile([P, H], U8, align_bytes=64)
        prm = const.tile([P, 16], F32)

        def weight_regroup(k):
            if k == 0:
                nc.scalar.copy(out=gwa[:], in_=w1sin[:, 0:4, :].rearrange("p t n -> p n t"))
            elif k == 1:
                nc.scalar.copy(out=gwb[:, :, 0], in_=w1sin[:, 4, :])
            elif k == 2:
                nc.scalar.copy(out=gwc[:, :, 0:3], in_=w1num[:].rearrange("p i n -> p n i"))
            else:
                nc.scalar.copy(out=gw2[:], in_=w2raw[:].rearrange("p t n -> p n t"))

        def weight_quantise(k):
            if k < 3:
                gw = (gwa, gwb, gwc)[k]
                nc.vector.quantize_mx(out=w1c[:, k, :].bitcast(FP8X4), scales=w1s[:, k, :],
                                      in_=gw[:].rearrange("p n t -> p (n t)"))
            else:
                nc.vector.quantize_mx(out=w2c[:].bitcast(FP8X4), scales=w2s[:],
                                      in_=gw2[:].rearrange("p n t -> p (n t)"))

        def number_params():
            cols_ps = psum.tile([P, P], BF16, tag="bank", name="cols_ps")
            nc.tensor.transpose(cols_ps[:], rows[:], ident[:])
            nc.vector.tensor_copy(out=prm[:, 0:14], in_=cols_ps[:, 0:14])

        n_t = {}
        f_t = {}
        planes_t = {}
        ga_t = {}
        a_t = {}
        fc_t = {}
        fs_t = {}
        apl_t = {}
        hg_t = {}
        hc_t = {}
        hs_t = {}
        ot_t = {}
        o_t = {}

        def xview(c):
            return xy_t[c][:].rearrange("p (b c) -> p b c", c=2)[:, :, 0]

        def v_int(c, s):
            n_t[s] = work.tile([P, F], I32, tag="n", name="n")
            nc.vector.tensor_scalar(out=n_t[s][:], in0=xview(c), scalar1=wt[:, s:s + 1], scalar2=bt[:, s:s + 1],
                                    op0=ALU.mult, op1=ALU.add)

        def v_frac(c, s):
            f_t[s] = work.tile([P, F], F32, tag="f", bufs=3, name="f")
            nc.vector.scalar_tensor_tensor(out=f_t[s][:], in0=xview(c), scalar=wt[:, s:s + 1], in1=n_t[s][:],
                                           op0=ALU.mult, op1=ALU.subtract)

        def s_sin(c, s):
            if s == 0:
                planes_t[c] = work.tile([P, 4, F], BF16, tag="planes", name="planes")
            dst = planes_t[c][:, s, :] if s < 4 else gb[:, :, 0]
            nc.scalar.activation(out=dst, in_=f_t[s][:], func=ACT.Sin, bias=beta[:, s:s + 1], scale=TWO_PI)

        def s_regroup(c):
            ga_t[c] = work.tile([P, F, 4], BF16, tag="ga", align_bytes=64, name="ga")
            nc.scalar.copy(out=ga_t[c][:].rearrange("p (c i) t -> p c t i", i=4),
                           in_=planes_t[c][:].rearrange("p t (c i) -> p c t i", i=4))

        def s_affine(c):
            a_t[c] = work.tile([P, 3, F], F32, tag="a", bufs=1, name="a")
            nc.scalar.activation(out=a_t[c][:, 2, :], in_=tin_t[c][:, 2, :], func=ACT.Identity,
                                 bias=prm[:, 5:6], scale=prm[:, 2:3])

        def v_affine(c):
            for i in range(2):
                nc.vector.tensor_scalar(out=a_t[c][:, i, :], in0=tin_t[c][:, i, :], scalar1=prm[:, i:i + 1],
                                        scalar2=prm[:, 3 + i:4 + i], op0=ALU.mult, op1=ALU.add)

        def v_number(c):
            a_v = a_t[c][:].rearrange("p i b -> p b i")
            nc.vector.scalar_tensor_tensor(out=gc[:, :, 0:3], in0=a_v, scalar=0.01, in1=a_v,
                                           op0=ALU.mult, op1=ALU.max)

        def v_quantise(c, q):
            g = (ga_t[c], gb, gc)[q]
            fc_t[(c, q)] = codes.tile([P, F], U32, name="fc%d" % q, align_bytes=64)
            fs_t[(c, q)] = codes.tile([P, F], U8, name="fs%d" % q, align_bytes=64)
            nc.vector.quantize_mx(out=fc_t[(c, q)][:].bitcast(FP8X4), scales=fs_t[(c, q)][:],
                                  in_=g[:].rearrange("p b t -> p (b t)"))

        def layer1(j):
            c = j // 2
            cs = slice(NT * (j % 2), NT * (j % 2) + NT)
            apl_t[j] = big.tile([P, 4, NT], F32, tag="apl", name="apl", align_bytes=64)
            for t in range(4):
                ms = slice(P * t, P * t + P)
                acc = psum.tile([P, NT], F32, tag="bank", name="acc")
                for q in range(3):
                    nc.tensor.matmul_mx(out=acc[:], lhsT=w1c[:, q, ms].bitcast(FP8X4), lhsT_scale=w1s[:, q, ms],
                                        rhs=fc_t[(c, q)][:, cs].bitcast(FP8X4), rhs_scale=fs_t[(c, q)][:, cs],
                                        start=(q == 0), stop=(q == 2))
                nc.scalar.activation(out=apl_t[j][:, t, :], in_=acc[:], func=ACT.Identity,
                                     bias=prm[:, 6 + t:7 + t], scale=1.0)

        def v_hidden(j):
            hg_t[j] = hid.tile([P, NT, 4], BF16, tag="hg", align_bytes=64, name="hg")
            apv = apl_t[j][:].rearrange("p t b -> p b t")
            nc.vector.scalar_tensor_tensor(out=hg_t[j][:], in0=apv, scalar=0.01, in1=apv, op0=ALU.mult, op1=ALU.max)

        def v_quantise_hidden(j):
            hc_t[j] = hid.tile([P, NT], U32, tag="hc", align_bytes=64, name="hc")
            hs_t[j] = hid.tile([P, NT], U8, tag="hs", align_bytes=64, name="hs")
            nc.vector.quantize_mx(out=hc_t[j][:].bitcast(FP8X4), scales=hs_t[j][:],
                                  in_=hg_t[j][:].rearrange("p b t -> p (b t)"))

        def layer2(j):
            ot_t[j] = big.tile([P, 4, NT], F32, tag="ot", name="ot", align_bytes=64)
            for m in range(4):
                ms = slice(P * m, P * m + P)
                acc2 = psum.tile([P, NT], F32, tag="bank", name="acc2")
                nc.tensor.matmul_mx(out=acc2[:], lhsT=w2c[:, ms].bitcast(FP8X4), lhsT_scale=w2s[:, ms],
                                    rhs=hc_t[j][:].bitcast(FP8X4), rhs_scale=hs_t[j][:], start=True, stop=True)
                nc.scalar.activation(out=ot_t[j][:, m, :], in_=acc2[:], func=ACT.Identity,
                                     bias=prm[:, 10 + m:11 + m], scale=1.0)

        def v_lrelu(j, i0, i1):
            o = ot_t[j][:, :, P * i0:P * i1]
            nc.vector.scalar_tensor_tensor(out=o, in0=o, scalar=0.01, in1=o, op0=ALU.mult, op1=ALU.max)

        def turn(j, i0, i1):
            if i0 == 0:
                o_t[j] = big.tile([P, 4, H], F32, tag="o", bufs=3, name="o", align_bytes=64)
            for i in range(i0, i1):
                tb = psum.tile([P, H], F32, tag="bank", name="tb")
                for m in range(4):
                    nc.tensor.transpose(tb[:, P * m:P * m + P], ot_t[j][:, m, P * i:P * i + P], ident32[:])
                nc.scalar.copy(out=o_t[j][:, i, :], in_=tb[:])
            lo = NT * j + P * i0
            hi = NT * j + P * i1
            nc.sync.dma_start(out=out[lo:hi, :].rearrange("(i p) n -> p i n", p=P), in_=o_t[j][:, i0:i1, :])

        for c in range(NCH + 1):
            feat = c < NCH
            back = c >= 1
            j0 = 2 * (c - 1)
            j1 = j0 + 1
            if c + 1 < NCH:
                load_xy(c + 1)
                load_tin(c + 1)
            if feat:
                v_int(c, 0)
                v_int(c, 1)
            if c == 0:
                weight_regroup(0)
                weight_regroup(1)
                number_params()
            if back:
                layer1(j0)
            if feat:
                v_frac(c, 0)
                s_sin(c, 0)
                v_int(c, 2)
            if c == 0:
                weight_regroup(2)
            if feat:
                v_frac(c, 1)
                s_sin(c, 1)
                v_int(c, 3)
            if c == 0:
                weight_regroup(3)
                weight_quantise(0)
            if back:
                layer1(j1)
            if feat:
                v_frac(c, 2)
                s_sin(c, 2)
            if c == 0:
                weight_quantise(1)
            if back:
                v_hidden(j0)
            if c >= 2:
                turn(j0 - 1, 0, 4)
            if feat:
                v_int(c, 4)
                v_frac(c, 3)
                s_sin(c, 3)
                s_affine(c)
            if c == 0:
                weight_quantise(2)
            if back:
                v_quantise_hidden(j0)
                layer2(j0)
            if feat:
                v_frac(c, 4)
                s_sin(c, 4)
                v_affine(c)
            if c == 0:
                weight_quantise(3)
            if back:
                v_hidden(j1)
            if feat:
                s_regroup(c)
                v_number(c)
            if back:
                v_quantise_hidden(j1)
                layer2(j1)
                v_lrelu(j0, 0, 4)
                turn(j0, 0, 4)
            if feat:
                v_quantise(c, 1)
                v_quantise(c, 2)
                v_quantise(c, 0)
            if back and feat:
                v_lrelu(j1, 0, 4)
        last = 2 * NCH - 1
        for i in range(4):
            v_lrelu(last, i, i + 1)
            turn(last, i, i + 1)
